import numpy as np
import ml_dtypes


def mxq(x, axis, fmt="e4m3"):
    dtype, down = {"e4m3": (ml_dtypes.float8_e4m3fn, 7), "e5m2": (ml_dtypes.float8_e5m2, 14)}[fmt]
    v = np.moveaxis(np.asarray(x, np.float32).astype(ml_dtypes.bfloat16).astype(np.float64), axis, -1)
    blocks = v.reshape(v.shape[:-1] + (-1, 32))
    amax = np.abs(blocks).max(-1, keepdims=True)
    byte = np.maximum(np.where(amax > 0, np.frexp(amax)[1] - 1 + 127, 0) - down, 1)
    scale = np.exp2(byte - 127.0)
    codes = (blocks / scale).astype(np.float32).astype(dtype).astype(np.float64)
    return np.moveaxis((codes * scale).reshape(v.shape), -1, axis)


WIDE = False


def mx_kscale(k):
    if not WIDE:
        return np.ones(k)
    levels = np.array([10, -10, 5, -5, 0])
    if k % 512:
        return np.exp2(np.random.permutation(np.resize(levels, k // 32))).repeat(32)
    a = np.empty((k // 512, 16))
    for p in range(k // 512):
        a[p, :8] = np.random.permutation(np.resize(levels, 8))
        for g in range(8):
            far = levels[np.abs(levels - a[p, g]) >= 10]
            a[p, g + 8] = far[np.random.randint(len(far))]
    return np.exp2(a.ravel()).repeat(32)


BF16 = ml_dtypes.bfloat16


def bf(x):
    return np.asarray(x, np.float32).astype(BF16)


def f64(x):
    return np.asarray(x).astype(np.float64)


B, S, D, E, R = 2, 256, 16384, 8, 64


def setup_inputs():
    s = mx_kscale(D)
    return {"x": bf(np.random.standard_normal((B, S, D)) * s),
            "W": bf(np.random.standard_normal((E, R, D)) * (1.0 / np.sqrt(D)) / s)}


def reference(x, W):
    xq = mxq(f64(x), 2, "e4m3")
    Wq = mxq(f64(W), 2, "e4m3")
    y = xq[None, :, :, :] @ Wq.transpose(0, 2, 1)[:, None, :, :]
    return tuple(y[e] for e in range(W.shape[0]))

@@ -1,0 +1,130 @@
+from contextlib import ExitStack
+
+import concourse.mybir as mybir
+from concourse.masks import make_identity
+
+BF16 = mybir.dt.bfloat16
+F32 = mybir.dt.float32
+U32 = mybir.dt.uint32
+U8 = mybir.dt.uint8
+FP8X4 = mybir.dt.float8_e4m3fn_x4
+
+P = 128
+D = 16384
+ROWS = 512
+EXPERTS = 8
+RANK = 64
+ROW_TILES = ROWS // P
+
+D_PASS = 4 * P
+PASSES = D // D_PASS
+WORDS_PASS = D_PASS // 2
+BANK_WORDS = 512
+BANKS_PASS = 2 * ROWS * WORDS_PASS // (P * BANK_WORDS)
+
+HEAD_PASSES = 8
+PASSES_PER_LOAD = 2
+LOADS_AHEAD = 7
+
+PASSES_PER_ROUND = 1
+ROUNDS = PASSES // PASSES_PER_ROUND
+LAG = 2
+
+FLOPS = 2 * ROWS * ROWS * D
+
+
+def tile_moelineara_k_kernel(tc, x, W, *outs):
+    nc = tc.nc
+
+    x_rows = x.flatten_outer_dims().rearrange("(p i) d -> p i d", i=ROW_TILES)
+    w_rows = W.flatten_outer_dims().rearrange("(j p) d -> p j d", p=P)
+
+    with ExitStack() as ctx:
+        ctx.enter_context(tc.manual_schedule())
+        fixed = ctx.enter_context(tc.tile_pool(name="fixed", bufs=1))
+        stage = ctx.enter_context(tc.tile_pool(name="stage", bufs=LOADS_AHEAD + 1))
+        group = ctx.enter_context(tc.tile_pool(name="group", bufs=3))
+        quant = ctx.enter_context(tc.tile_pool(name="quant", bufs=(LAG + 1) * PASSES_PER_ROUND + 1))
+        turned = ctx.enter_context(tc.psum_pool(name="turned", bufs=BANKS_PASS))
+        sums = ctx.enter_context(tc.psum_pool(name="sums", bufs=1))
+
+        ident = fixed.tile([P, P], F32, name="ident")
+        make_identity(nc, ident[:])
+
+        acc = [sums.tile([P, ROWS], F32, name="acc%d" % i) for i in range(ROW_TILES)]
+
+        def load(first_pass, count):
+            x_stage = stage.tile([P, ROW_TILES, PASSES_PER_LOAD * D_PASS], BF16, name="x_stage")
+            w_stage = stage.tile([P, ROW_TILES, PASSES_PER_LOAD * D_PASS], BF16, name="w_stage")
+            columns = slice(first_pass * D_PASS, (first_pass + count) * D_PASS)
+            nc.sync.dma_start(out=x_stage[:, :, : count * D_PASS], in_=x_rows[:, :, columns])
+            nc.sync.dma_start(out=w_stage[:, :, : count * D_PASS], in_=w_rows[:, :, columns])
+            return x_stage, w_stage
+
+        def turn_and_quantise(pair, c):
+            grouped = group.tile([P, 2 * ROWS * 4], BF16, name="grouped", align_bytes=64)
+            grouped_words = grouped[:].bitcast(F32)
+            for b in range(BANKS_PASS):
+                operand = pair[b // 2]
+                bank = turned.tile([P, 2, 2 * P], F32, name="bank")
+                for j in range(2):
+                    words = operand[:, 2 * (b % 2) + j, :].bitcast(F32)
+                    for u in range(2):
+                        first = WORDS_PASS * c + u
+                        nc.tensor.transpose(
+                            bank[:, u, P * j : P * (j + 1)],
+                            words[:, first : WORDS_PASS * (c + 1) : 2],
+                            ident[:],
+                        )
+                copy = nc.vector.tensor_copy if b == BANKS_PASS - 1 else nc.scalar.copy
+                copy(
+                    out=grouped_words[:, BANK_WORDS * b : BANK_WORDS * (b + 1)].rearrange(
+                        "p (c u) -> p c u", u=2
+                    ),
+                    in_=bank[:].rearrange("p u c -> p c u"),
+                )
+            codes = quant.tile([P, 2 * ROWS], U32, name="codes", align_bytes=64)
+            scales = quant.tile([P, 2 * ROWS], U8, name="scales", align_bytes=64)
+            nc.vector.quantize_mx(out=codes[:].bitcast(FP8X4), scales=scales[:], in_=grouped[:])
+            return codes, scales
+
+        def multiply(g, codes, scales):
+            for i in range(ROW_TILES):
+                tokens = slice(P * i, P * (i + 1))
+                nc.tensor.matmul_mx(
+                    out=acc[i][:],
+                    lhsT=codes[:, tokens].bitcast(FP8X4),
+                    lhsT_scale=scales[:, tokens],
+                    rhs=codes[:, ROWS : 2 * ROWS].bitcast(FP8X4),
+                    rhs_scale=scales[:, ROWS : 2 * ROWS],
+                    start=(g == 0),
+                    stop=(g == PASSES - 1),
+                )
+
+        loads = [(g, 1) for g in range(HEAD_PASSES)]
+        loads.extend([(g, PASSES_PER_LOAD) for g in range(HEAD_PASSES, PASSES, PASSES_PER_LOAD)])
+        home = [(n, c) for n, (first_pass, count) in enumerate(loads) for c in range(count)]
+
+        staged = []
+        quantised = []
+        for round_no in range(ROUNDS + LAG):
+            if round_no < ROUNDS:
+                for g in range(round_no * PASSES_PER_ROUND, (round_no + 1) * PASSES_PER_ROUND):
+                    n, c = home[g]
+                    for ahead in range(len(staged), min(n + LOADS_AHEAD + 1, len(loads))):
+                        staged.append(load(loads[ahead][0], loads[ahead][1]))
+                    quantised.append(turn_and_quantise(staged[n], c))
+            if round_no >= LAG:
+                late = round_no - LAG
+                for g in range(late * PASSES_PER_ROUND, (late + 1) * PASSES_PER_ROUND):
+                    multiply(g, quantised[g][0], quantised[g][1])
+
+        result = fixed.tile([P, EXPERTS, ROW_TILES, RANK], F32, name="result")
+        for i in range(ROW_TILES):
+            copy = nc.scalar.copy if i % 2 == 0 else nc.vector.tensor_copy
+            copy(out=result[:, :, i, :], in_=acc[i][:].rearrange("p (e r) -> p e r", e=EXPERTS))
+        for e in range(EXPERTS):
+            nc.sync.dma_start(
+                out=outs[e].flatten_outer_dims().rearrange("(p i) r -> p i r", i=ROW_TILES),
+                in_=result[:, e, :, :],
+            )

@@ -26,8 +26,7 @@ HEAD_PASSES = 8
 PASSES_PER_LOAD = 2
 LOADS_AHEAD = 7
 
-PASSES_PER_ROUND = 1
-ROUNDS = PASSES // PASSES_PER_ROUND
+SPLIT_AHEAD = 2
 LAG = 2
 
 FLOPS = 2 * ROWS * ROWS * D
@@ -43,8 +42,9 @@ def tile_moelineara_k_kernel(tc, x, W, *outs):
         ctx.enter_context(tc.manual_schedule())
         fixed = ctx.enter_context(tc.tile_pool(name="fixed", bufs=1))
         stage = ctx.enter_context(tc.tile_pool(name="stage", bufs=LOADS_AHEAD + 1))
+        split = ctx.enter_context(tc.tile_pool(name="split", bufs=SPLIT_AHEAD + 2))
         group = ctx.enter_context(tc.tile_pool(name="group", bufs=3))
-        quant = ctx.enter_context(tc.tile_pool(name="quant", bufs=(LAG + 1) * PASSES_PER_ROUND + 1))
+        quant = ctx.enter_context(tc.tile_pool(name="quant", bufs=LAG + 2))
         turned = ctx.enter_context(tc.psum_pool(name="turned", bufs=BANKS_PASS))
         sums = ctx.enter_context(tc.psum_pool(name="sums", bufs=1))
 
@@ -61,28 +61,37 @@ def tile_moelineara_k_kernel(tc, x, W, *outs):
             nc.sync.dma_start(out=w_stage[:, :, : count * D_PASS], in_=w_rows[:, :, columns])
             return x_stage, w_stage
 
-        def turn_and_quantise(pair, c):
+        def split_words(pair, c):
+            halves = []
+            for operand, name in zip(pair, ("x_split", "w_split")):
+                parted = split.tile([P, ROW_TILES, 2, P], F32, name=name, align_bytes=64)
+                words = operand[:].bitcast(F32)[:, :, WORDS_PASS * c : WORDS_PASS * (c + 1)]
+                nc.vector.tensor_copy(out=parted[:], in_=words.rearrange("p j (q u) -> p j u q", u=2))
+                halves.append(parted)
+            return halves
+
+        def turn(halves):
             grouped = group.tile([P, 2 * ROWS * 4], BF16, name="grouped", align_bytes=64)
             grouped_words = grouped[:].bitcast(F32)
             for b in range(BANKS_PASS):
-                operand = pair[b // 2]
+                operand = halves[b // 2]
                 bank = turned.tile([P, 2, 2 * P], F32, name="bank")
                 for j in range(2):
-                    words = operand[:, 2 * (b % 2) + j, :].bitcast(F32)
                     for u in range(2):
-                        first = WORDS_PASS * c + u
                         nc.tensor.transpose(
                             bank[:, u, P * j : P * (j + 1)],
-                            words[:, first : WORDS_PASS * (c + 1) : 2],
+                            operand[:, 2 * (b % 2) + j, u, :],
                             ident[:],
                         )
-                copy = nc.vector.tensor_copy if b == BANKS_PASS - 1 else nc.scalar.copy
-                copy(
+                nc.scalar.copy(
                     out=grouped_words[:, BANK_WORDS * b : BANK_WORDS * (b + 1)].rearrange(
                         "p (c u) -> p c u", u=2
                     ),
                     in_=bank[:].rearrange("p u c -> p c u"),
                 )
+            return grouped
+
+        def quantise(grouped):
             codes = quant.tile([P, 2 * ROWS], U32, name="codes", align_bytes=64)
             scales = quant.tile([P, 2 * ROWS], U8, name="scales", align_bytes=64)
             nc.vector.quantize_mx(out=codes[:].bitcast(FP8X4), scales=scales[:], in_=grouped[:])
@@ -106,18 +115,21 @@ def tile_moelineara_k_kernel(tc, x, W, *outs):
         home = [(n, c) for n, (first_pass, count) in enumerate(loads) for c in range(count)]
 
         staged = []
+        parted = []
+        grouped = []
         quantised = []
-        for round_no in range(ROUNDS + LAG):
-            if round_no < ROUNDS:
-                for g in range(round_no * PASSES_PER_ROUND, (round_no + 1) * PASSES_PER_ROUND):
-                    n, c = home[g]
-                    for ahead in range(len(staged), min(n + LOADS_AHEAD + 1, len(loads))):
-                        staged.append(load(loads[ahead][0], loads[ahead][1]))
-                    quantised.append(turn_and_quantise(staged[n], c))
-            if round_no >= LAG:
-                late = round_no - LAG
-                for g in range(late * PASSES_PER_ROUND, (late + 1) * PASSES_PER_ROUND):
-                    multiply(g, quantised[g][0], quantised[g][1])
+        for g in range(PASSES + LAG):
+            if 1 <= g <= PASSES:
+                quantised.append(quantise(grouped[g - 1]))
+            while len(parted) < min(g + SPLIT_AHEAD + 1, PASSES):
+                n, c = home[len(parted)]
+                for ahead in range(len(staged), min(n + LOADS_AHEAD + 1, len(loads))):
+                    staged.append(load(loads[ahead][0], loads[ahead][1]))
+                parted.append(split_words(staged[n], c))
+            if g < PASSES:
+                grouped.append(turn(parted[g]))
+            if g >= LAG:
+                multiply(g - LAG, quantised[g - LAG][0], quantised[g - LAG][1])
 
         result = fixed.tile([P, EXPERTS, ROW_TILES, RANK], F32, name="result")
         for i in range(ROW_TILES):

@@ -66,7 +66,10 @@ def tile_moelineara_k_kernel(tc, x, W, *outs):
             for operand, name in zip(pair, ("x_split", "w_split")):
                 parted = split.tile([P, ROW_TILES, 2, P], F32, name=name, align_bytes=64)
                 words = operand[:].bitcast(F32)[:, :, WORDS_PASS * c : WORDS_PASS * (c + 1)]
-                nc.vector.tensor_copy(out=parted[:], in_=words.rearrange("p j (q u) -> p j u q", u=2))
+                nc.vector.tensor_copy(
+                    out=parted[:].rearrange("p j u (s w) -> p j u s w", w=8),
+                    in_=words.rearrange("p j (s u w) -> p j u s w", u=2, w=8),
+                )
                 halves.append(parted)
             return halves
 

@@ -26,8 +26,8 @@ HEAD_PASSES = 8
 PASSES_PER_LOAD = 2
 LOADS_AHEAD = 7
 
-SPLIT_AHEAD = 2
-LAG = 2
+EARLY = 4
+LATER = 5
 
 FLOPS = 2 * ROWS * ROWS * D
 
@@ -42,9 +42,9 @@ def tile_moelineara_k_kernel(tc, x, W, *outs):
         ctx.enter_context(tc.manual_schedule())
         fixed = ctx.enter_context(tc.tile_pool(name="fixed", bufs=1))
         stage = ctx.enter_context(tc.tile_pool(name="stage", bufs=LOADS_AHEAD + 1))
-        split = ctx.enter_context(tc.tile_pool(name="split", bufs=SPLIT_AHEAD + 2))
+        split = ctx.enter_context(tc.tile_pool(name="split", bufs=4))
         group = ctx.enter_context(tc.tile_pool(name="group", bufs=3))
-        quant = ctx.enter_context(tc.tile_pool(name="quant", bufs=LAG + 2))
+        quant = ctx.enter_context(tc.tile_pool(name="quant", bufs=4))
         turned = ctx.enter_context(tc.psum_pool(name="turned", bufs=BANKS_PASS))
         sums = ctx.enter_context(tc.psum_pool(name="sums", bufs=1))
 
@@ -54,39 +54,48 @@ def tile_moelineara_k_kernel(tc, x, W, *outs):
         acc = [sums.tile([P, ROWS], F32, name="acc%d" % i) for i in range(ROW_TILES)]
 
         def load(first_pass, count):
-            x_stage = stage.tile([P, ROW_TILES, PASSES_PER_LOAD * D_PASS], BF16, name="x_stage")
-            w_stage = stage.tile([P, ROW_TILES, PASSES_PER_LOAD * D_PASS], BF16, name="w_stage")
             columns = slice(first_pass * D_PASS, (first_pass + count) * D_PASS)
-            nc.sync.dma_start(out=x_stage[:, :, : count * D_PASS], in_=x_rows[:, :, columns])
-            nc.sync.dma_start(out=w_stage[:, :, : count * D_PASS], in_=w_rows[:, :, columns])
-            return x_stage, w_stage
+            pieces = []
+            for rows, name in ((x_rows, "x_stage"), (w_rows, "w_stage")):
+                if first_pass == 0:
+                    for j in range(0, ROW_TILES, 2):
+                        first = fixed.tile([P, 2, D_PASS], BF16, name="%s%d" % (name, j))
+                        nc.sync.dma_start(out=first[:], in_=rows[:, j : j + 2, columns])
+                        pieces.append(first)
+                else:
+                    staged = stage.tile([P, ROW_TILES, PASSES_PER_LOAD * D_PASS], BF16, name=name)
+                    nc.sync.dma_start(out=staged[:, :, : count * D_PASS], in_=rows[:, :, columns])
+                    pieces.append(staged)
+            return [
+                [piece[:].bitcast(F32)[:, :, WORDS_PASS * c : WORDS_PASS * (c + 1)] for piece in pieces]
+                for c in range(count)
+            ]
 
-        def split_words(pair, c):
-            halves = []
-            for operand, name in zip(pair, ("x_split", "w_split")):
-                parted = split.tile([P, ROW_TILES, 2, P], F32, name=name, align_bytes=64)
-                words = operand[:].bitcast(F32)[:, :, WORDS_PASS * c : WORDS_PASS * (c + 1)]
+        def split_words(pieces):
+            row_tiles = []
+            for n, words in enumerate(pieces):
+                tiles = words.shape[1]
+                pool = fixed if tiles == 2 else split
+                parted = pool.tile([P, tiles, 2, P], F32, name="split%d_%d" % (tiles, n), align_bytes=64)
                 nc.vector.tensor_copy(
                     out=parted[:].rearrange("p j u (s w) -> p j u s w", w=8),
                     in_=words.rearrange("p j (s u w) -> p j u s w", u=2, w=8),
                 )
-                halves.append(parted)
-            return halves
+                row_tiles.extend([parted[:, j, :, :] for j in range(tiles)])
+            return row_tiles
 
-        def turn(halves):
+        def turn(row_tiles, last):
             grouped = group.tile([P, 2 * ROWS * 4], BF16, name="grouped", align_bytes=64)
             grouped_words = grouped[:].bitcast(F32)
-            for b in range(BANKS_PASS):
-                operand = halves[b // 2]
+            for b in (2, 3, 0, 1) if last else range(BANKS_PASS):
                 bank = turned.tile([P, 2, 2 * P], F32, name="bank")
                 for j in range(2):
                     for u in range(2):
                         nc.tensor.transpose(
-                            bank[:, u, P * j : P * (j + 1)],
-                            operand[:, 2 * (b % 2) + j, u, :],
-                            ident[:],
+                            bank[:, u, P * j : P * (j + 1)], row_tiles[2 * b + j][:, u, :], ident[:]
                         )
-                nc.scalar.copy(
+                copy = nc.vector.tensor_copy if last and b == 3 else nc.scalar.copy
+                copy(
                     out=grouped_words[:, BANK_WORDS * b : BANK_WORDS * (b + 1)].rearrange(
                         "p (c u) -> p c u", u=2
                     ),
@@ -94,52 +103,73 @@ def tile_moelineara_k_kernel(tc, x, W, *outs):
                 )
             return grouped
 
-        def quantise(grouped):
+        def quantise(grouped, parts):
             codes = quant.tile([P, 2 * ROWS], U32, name="codes", align_bytes=64)
             scales = quant.tile([P, 2 * ROWS], U8, name="scales", align_bytes=64)
-            nc.vector.quantize_mx(out=codes[:].bitcast(FP8X4), scales=scales[:], in_=grouped[:])
+            for first, end in parts:
+                nc.vector.quantize_mx(
+                    out=codes[:, first:end].bitcast(FP8X4),
+                    scales=scales[:, first:end],
+                    in_=grouped[:, 4 * first : 4 * end],
+                )
             return codes, scales
 
-        def multiply(g, codes, scales):
-            for i in range(ROW_TILES):
-                tokens = slice(P * i, P * (i + 1))
-                nc.tensor.matmul_mx(
-                    out=acc[i][:],
-                    lhsT=codes[:, tokens].bitcast(FP8X4),
-                    lhsT_scale=scales[:, tokens],
-                    rhs=codes[:, ROWS : 2 * ROWS].bitcast(FP8X4),
-                    rhs_scale=scales[:, ROWS : 2 * ROWS],
-                    start=(g == 0),
-                    stop=(g == PASSES - 1),
-                )
+        def multiply(g, i):
+            codes, scales = quantised[g]
+            tokens = slice(P * i, P * (i + 1))
+            nc.tensor.matmul_mx(
+                out=acc[i][:],
+                lhsT=codes[:, tokens].bitcast(FP8X4),
+                lhsT_scale=scales[:, tokens],
+                rhs=codes[:, ROWS : 2 * ROWS].bitcast(FP8X4),
+                rhs_scale=scales[:, ROWS : 2 * ROWS],
+                start=(g == 0),
+                stop=(g == PASSES - 1),
+            )
 
         loads = [(g, 1) for g in range(HEAD_PASSES)]
         loads.extend([(g, PASSES_PER_LOAD) for g in range(HEAD_PASSES, PASSES, PASSES_PER_LOAD)])
         home = [(n, c) for n, (first_pass, count) in enumerate(loads) for c in range(count)]
 
+        products = [(g, i) for g in range(PASSES - 2) for i in range(ROW_TILES)]
+        products.extend([(g, i) for i0 in (0, 2) for g in (PASSES - 2, PASSES - 1) for i in (i0, i0 + 1)])
+
         staged = []
         parted = []
         grouped = []
         quantised = []
-        for g in range(PASSES + LAG):
-            if 1 <= g <= PASSES:
-                quantised.append(quantise(grouped[g - 1]))
-            while len(parted) < min(g + SPLIT_AHEAD + 1, PASSES):
+        done = 0
+        for g in range(PASSES):
+            if g > 0:
+                quantised.append(quantise(grouped[g - 1], [(0, 2 * ROWS)]))
+            while len(parted) < min(g + (2 if g < EARLY else 3), PASSES):
                 n, c = home[len(parted)]
                 for ahead in range(len(staged), min(n + LOADS_AHEAD + 1, len(loads))):
                     staged.append(load(loads[ahead][0], loads[ahead][1]))
-                parted.append(split_words(staged[n], c))
-            if g < PASSES:
-                grouped.append(turn(parted[g]))
-            if g >= LAG:
-                multiply(g - LAG, quantised[g - LAG][0], quantised[g - LAG][1])
+                parted.append(split_words(staged[n][c]))
+            grouped.append(turn(parted[g], g == PASSES - 1))
+            if g > 0:
+                count = ROW_TILES - 1 if LATER <= g < LATER + ROW_TILES else ROW_TILES
+                for pass_no, i in products[done : done + count]:
+                    multiply(pass_no, i)
+                done += count
+        quantised.append(quantise(grouped[PASSES - 1], [(ROWS, 2 * ROWS), (0, 2 * P), (2 * P, ROWS)]))
+        for pass_no, i in products[done:]:
+            multiply(pass_no, i)
 
-        result = fixed.tile([P, EXPERTS, ROW_TILES, RANK], F32, name="result")
-        for i in range(ROW_TILES):
-            copy = nc.scalar.copy if i % 2 == 0 else nc.vector.tensor_copy
-            copy(out=result[:, :, i, :], in_=acc[i][:].rearrange("p (e r) -> p e r", e=EXPERTS))
-        for e in range(EXPERTS):
-            nc.sync.dma_start(
-                out=outs[e].flatten_outer_dims().rearrange("(p i) r -> p i r", i=ROW_TILES),
-                in_=result[:, e, :, :],
-            )
+        for half in range(2):
+            result = fixed.tile([P, EXPERTS, 2, RANK], F32, name="result%d" % half)
+            for j in range(2):
+                copy = nc.scalar.copy if j == 0 else nc.vector.tensor_copy
+                copy(
+                    out=result[:, :, j, :],
+                    in_=acc[2 * half + j][:].rearrange("p (e r) -> p e r", e=EXPERTS),
+                )
+            for e in range(EXPERTS):
+                queue = nc.scalar if half == 1 and e % 2 == 1 else nc.sync
+                queue.dma_start(
+                    out=outs[e].flatten_outer_dims().rearrange("(p i) r -> p i r", i=ROW_TILES)[
+                        :, 2 * half : 2 * half + 2, :
+                    ],
+                    in_=result[:, e, :, :],
+                )

@@ -26,6 +26,9 @@ HEAD_PASSES = 8
 PASSES_PER_LOAD = 2
 LOADS_AHEAD = 7
 
+SHORT_TURNS = 9
+LONG_TURN = 6
+
 EARLY = 4
 LATER = 5
 
@@ -84,24 +87,15 @@ def tile_moelineara_k_kernel(tc, x, W, *outs):
                 row_tiles.extend([parted[:, j, :, :] for j in range(tiles)])
             return row_tiles
 
-        def turn(row_tiles, last):
-            grouped = group.tile([P, 2 * ROWS * 4], BF16, name="grouped", align_bytes=64)
-            grouped_words = grouped[:].bitcast(F32)
-            for b in (2, 3, 0, 1) if last else range(BANKS_PASS):
-                bank = turned.tile([P, 2, 2 * P], F32, name="bank")
-                for j in range(2):
-                    for u in range(2):
-                        nc.tensor.transpose(
-                            bank[:, u, P * j : P * (j + 1)], row_tiles[2 * b + j][:, u, :], ident[:]
-                        )
-                copy = nc.vector.tensor_copy if last and b == 3 else nc.scalar.copy
-                copy(
-                    out=grouped_words[:, BANK_WORDS * b : BANK_WORDS * (b + 1)].rearrange(
-                        "p (c u) -> p c u", u=2
-                    ),
-                    in_=bank[:].rearrange("p u c -> p c u"),
-                )
-            return grouped
+        def transpose_bank(row_tiles, b, grouped, copy):
+            bank = turned.tile([P, 2, 2 * P], F32, name="bank")
+            for j in range(2):
+                for u in range(2):
+                    nc.tensor.transpose(
+                        bank[:, u, P * j : P * (j + 1)], row_tiles[2 * b + j][:, u, :], ident[:]
+                    )
+            words = grouped[:].bitcast(F32)[:, BANK_WORDS * b : BANK_WORDS * (b + 1)]
+            copy(out=words.rearrange("p (c u) -> p c u", u=2), in_=bank[:].rearrange("p u c -> p c u"))
 
         def quantise(grouped, parts):
             codes = quant.tile([P, 2 * ROWS], U32, name="codes", align_bytes=64)
@@ -134,12 +128,23 @@ def tile_moelineara_k_kernel(tc, x, W, *outs):
         products = [(g, i) for g in range(PASSES - 2) for i in range(ROW_TILES)]
         products.extend([(g, i) for i0 in (0, 2) for g in (PASSES - 2, PASSES - 1) for i in (i0, i0 + 1)])
 
+        turns = []
+        banks = 0
+        while banks < PASSES * BANKS_PASS:
+            n = len(turns)
+            is_long = n >= SHORT_TURNS and banks < (PASSES - 2) * BANKS_PASS
+            banks += LONG_TURN if is_long else BANKS_PASS
+            left_out = BANKS_PASS if n == 0 else 1 if LATER <= n < LATER + 4 else 0
+            turns.append((banks, (LONG_TURN if is_long else BANKS_PASS) - left_out))
+
         staged = []
         parted = []
         grouped = []
         quantised = []
         done = 0
+        banks = 0
         for g in range(PASSES):
+            last = g == PASSES - 1
             if g > 0:
                 quantised.append(quantise(grouped[g - 1], [(0, 2 * ROWS)]))
             while len(parted) < min(g + (2 if g < EARLY else 3), PASSES):
@@ -147,29 +152,37 @@ def tile_moelineara_k_kernel(tc, x, W, *outs):
                 for ahead in range(len(staged), min(n + LOADS_AHEAD + 1, len(loads))):
                     staged.append(load(loads[ahead][0], loads[ahead][1]))
                 parted.append(split_words(staged[n][c]))
-            grouped.append(turn(parted[g], g == PASSES - 1))
-            if g > 0:
-                count = ROW_TILES - 1 if LATER <= g < LATER + ROW_TILES else ROW_TILES
-                for pass_no, i in products[done : done + count]:
-                    multiply(pass_no, i)
-                done += count
+            grouped.append(group.tile([P, 2 * ROWS * 4], BF16, name="grouped", align_bytes=64))
+            for b in (2, 3, 0, 1) if last else range(BANKS_PASS):
+                copy = nc.vector.tensor_copy if last and b == 3 else nc.scalar.copy
+                transpose_bank(parted[g], b, grouped[g], copy)
+                banks += 1
+                if banks == turns[0][0]:
+                    count = turns[0][1]
+                    for pass_no, i in products[done : done + count]:
+                        multiply(pass_no, i)
+                    done += count
+                    turns.remove(turns[0])
         quantised.append(quantise(grouped[PASSES - 1], [(ROWS, 2 * ROWS), (0, 2 * P), (2 * P, ROWS)]))
         for pass_no, i in products[done:]:
             multiply(pass_no, i)
 
-        for half in range(2):
-            result = fixed.tile([P, EXPERTS, 2, RANK], F32, name="result%d" % half)
-            for j in range(2):
-                copy = nc.scalar.copy if j == 0 else nc.vector.tensor_copy
-                copy(
-                    out=result[:, :, j, :],
-                    in_=acc[2 * half + j][:].rearrange("p (e r) -> p e r", e=EXPERTS),
-                )
-            for e in range(EXPERTS):
-                queue = nc.scalar if half == 1 and e % 2 == 1 else nc.sync
-                queue.dma_start(
-                    out=outs[e].flatten_outer_dims().rearrange("(p i) r -> p i r", i=ROW_TILES)[
-                        :, 2 * half : 2 * half + 2, :
-                    ],
-                    in_=result[:, e, :, :],
-                )
+        result = fixed.tile([P, EXPERTS, ROW_TILES, RANK], F32, name="result")
+        last = ROW_TILES - 1
+        for copy, i, first, end in (
+            (nc.scalar.copy, 0, 0, EXPERTS),
+            (nc.vector.tensor_copy, 1, 0, EXPERTS),
+            (nc.scalar.copy, 2, 0, EXPERTS),
+            (nc.vector.tensor_copy, last, 0, EXPERTS // 2),
+            (nc.scalar.copy, last, EXPERTS // 2, EXPERTS),
+        ):
+            copy(
+                out=result[:, first:end, i, :],
+                in_=acc[i][:, RANK * first : RANK * end].rearrange("p (e r) -> p e r", r=RANK),
+            )
+        for e in range(EXPERTS):
+            queue = nc.scalar if e >= EXPERTS // 2 and e % 2 == 1 else nc.sync
+            queue.dma_start(
+                out=outs[e].flatten_outer_dims().rearrange("(p i) r -> p i r", i=ROW_TILES),
+                in_=result[:, e, :, :],
+            )

@@ -26,11 +26,11 @@ HEAD_PASSES = 8
 PASSES_PER_LOAD = 2
 LOADS_AHEAD = 7
 
-SHORT_TURNS = 9
-LONG_TURN = 6
 
 EARLY = 4
 LATER = 5
+
+VECTOR_BANK = 2
 
 FLOPS = 2 * ROWS * ROWS * D
 
@@ -128,41 +128,35 @@ def tile_moelineara_k_kernel(tc, x, W, *outs):
         products = [(g, i) for g in range(PASSES - 2) for i in range(ROW_TILES)]
         products.extend([(g, i) for i0 in (0, 2) for g in (PASSES - 2, PASSES - 1) for i in (i0, i0 + 1)])
 
-        turns = []
-        banks = 0
-        while banks < PASSES * BANKS_PASS:
-            n = len(turns)
-            is_long = n >= SHORT_TURNS and banks < (PASSES - 2) * BANKS_PASS
-            banks += LONG_TURN if is_long else BANKS_PASS
-            left_out = BANKS_PASS if n == 0 else 1 if LATER <= n < LATER + 4 else 0
-            turns.append((banks, (LONG_TURN if is_long else BANKS_PASS) - left_out))
-
         staged = []
         parted = []
         grouped = []
         quantised = []
         done = 0
-        banks = 0
-        for g in range(PASSES):
-            last = g == PASSES - 1
-            if g > 0:
-                quantised.append(quantise(grouped[g - 1], [(0, 2 * ROWS)]))
-            while len(parted) < min(g + (2 if g < EARLY else 3), PASSES):
+
+        def split_up_to(end):
+            while len(parted) < min(end, PASSES):
                 n, c = home[len(parted)]
                 for ahead in range(len(staged), min(n + LOADS_AHEAD + 1, len(loads))):
                     staged.append(load(loads[ahead][0], loads[ahead][1]))
                 parted.append(split_words(staged[n][c]))
+
+        split_up_to(1)
+        for g in range(PASSES):
+            last = g == PASSES - 1
+            if g > 0:
+                quantised.append(quantise(grouped[g - 1], [(0, 2 * ROWS)]))
             grouped.append(group.tile([P, 2 * ROWS * 4], BF16, name="grouped", align_bytes=64))
             for b in (2, 3, 0, 1) if last else range(BANKS_PASS):
-                copy = nc.vector.tensor_copy if last and b == 3 else nc.scalar.copy
+                by_vector = b == VECTOR_BANK and g % 2 == 1
+                copy = nc.vector.tensor_copy if by_vector else nc.scalar.copy
                 transpose_bank(parted[g], b, grouped[g], copy)
-                banks += 1
-                if banks == turns[0][0]:
-                    count = turns[0][1]
-                    for pass_no, i in products[done : done + count]:
-                        multiply(pass_no, i)
-                    done += count
-                    turns.remove(turns[0])
+            split_up_to(g + (2 if g < EARLY else 3))
+            if g > 0:
+                count = ROW_TILES - 1 if LATER <= g < LATER + ROW_TILES else ROW_TILES
+                for pass_no, i in products[done : done + count]:
+                    multiply(pass_no, i)
+                done += count
         quantised.append(quantise(grouped[PASSES - 1], [(ROWS, 2 * ROWS), (0, 2 * P), (2 * P, ROWS)]))
         for pass_no, i in products[done:]:
             multiply(pass_no, i)

@@ -22,15 +22,13 @@ WORDS_PASS = D_PASS // 2
 BANK_WORDS = 512
 BANKS_PASS = 2 * ROWS * WORDS_PASS // (P * BANK_WORDS)
 
-HEAD_PASSES = 8
-PASSES_PER_LOAD = 2
-LOADS_AHEAD = 7
+SINGLES = 3
+STAGE_BUFS = 8
 
-
-EARLY = 4
+EARLY = 8
 LATER = 5
 
-VECTOR_BANK = 2
+VECTOR_BANK = 1
 
 FLOPS = 2 * ROWS * ROWS * D
 
@@ -44,7 +42,7 @@ def tile_moelineara_k_kernel(tc, x, W, *outs):
     with ExitStack() as ctx:
         ctx.enter_context(tc.manual_schedule())
         fixed = ctx.enter_context(tc.tile_pool(name="fixed", bufs=1))
-        stage = ctx.enter_context(tc.tile_pool(name="stage", bufs=LOADS_AHEAD + 1))
+        stage = ctx.enter_context(tc.tile_pool(name="stage", bufs=STAGE_BUFS))
         split = ctx.enter_context(tc.tile_pool(name="split", bufs=4))
         group = ctx.enter_context(tc.tile_pool(name="group", bufs=3))
         quant = ctx.enter_context(tc.tile_pool(name="quant", bufs=4))
@@ -56,57 +54,59 @@ def tile_moelineara_k_kernel(tc, x, W, *outs):
 
         acc = [sums.tile([P, ROWS], F32, name="acc%d" % i) for i in range(ROW_TILES)]
 
-        def load(first_pass, count):
+        def load(operand, first_pass, count):
+            rows = (x_rows, w_rows)[operand]
             columns = slice(first_pass * D_PASS, (first_pass + count) * D_PASS)
-            pieces = []
-            for rows, name in ((x_rows, "x_stage"), (w_rows, "w_stage")):
-                if first_pass == 0:
-                    for j in range(0, ROW_TILES, 2):
-                        first = fixed.tile([P, 2, D_PASS], BF16, name="%s%d" % (name, j))
-                        nc.sync.dma_start(out=first[:], in_=rows[:, j : j + 2, columns])
-                        pieces.append(first)
-                else:
-                    staged = stage.tile([P, ROW_TILES, PASSES_PER_LOAD * D_PASS], BF16, name=name)
-                    nc.sync.dma_start(out=staged[:, :, : count * D_PASS], in_=rows[:, :, columns])
-                    pieces.append(staged)
-            return [
-                [piece[:].bitcast(F32)[:, :, WORDS_PASS * c : WORDS_PASS * (c + 1)] for piece in pieces]
-                for c in range(count)
-            ]
+            if first_pass == 0:
+                staged = [
+                    fixed.tile([P, 2, D_PASS], BF16, name="first%d_%d" % (operand, j)) for j in (0, 2)
+                ]
+            else:
+                staged = [stage.tile([P, ROW_TILES, count * D_PASS], BF16, name="stage%d" % operand)]
+            tiles = ROW_TILES // len(staged)
+            for n, piece in enumerate(staged):
+                nc.sync.dma_start(out=piece[:], in_=rows[:, tiles * n : tiles * (n + 1), columns])
+            for c in range(count):
+                words = slice(WORDS_PASS * c, WORDS_PASS * (c + 1))
+                pieces[operand].append([piece[:].bitcast(F32)[:, :, words] for piece in staged])
 
-        def split_words(pieces):
-            row_tiles = []
-            for n, words in enumerate(pieces):
+        def split_words(operand, g):
+            for n, words in enumerate(pieces[operand][g]):
                 tiles = words.shape[1]
-                pool = fixed if tiles == 2 else split
-                parted = pool.tile([P, tiles, 2, P], F32, name="split%d_%d" % (tiles, n), align_bytes=64)
+                if g == 0:
+                    parted = fixed.tile(
+                        [P, tiles, 2, P], F32, name="split%d_%d" % (operand, n), align_bytes=64
+                    )
+                else:
+                    parted = split.tile([P, tiles, 2, P], F32, name="split%d" % operand, align_bytes=64)
                 nc.vector.tensor_copy(
                     out=parted[:].rearrange("p j u (s w) -> p j u s w", w=8),
                     in_=words.rearrange("p j (s u w) -> p j u s w", u=2, w=8),
                 )
-                row_tiles.extend([parted[:, j, :, :] for j in range(tiles)])
-            return row_tiles
+                row_tiles[g].extend([parted[:, j, :, :] for j in range(tiles)])
 
-        def transpose_bank(row_tiles, b, grouped, copy):
+        def transpose_bank(g, b, copy):
             bank = turned.tile([P, 2, 2 * P], F32, name="bank")
             for j in range(2):
                 for u in range(2):
                     nc.tensor.transpose(
-                        bank[:, u, P * j : P * (j + 1)], row_tiles[2 * b + j][:, u, :], ident[:]
+                        bank[:, u, P * j : P * (j + 1)], row_tiles[g][2 * b + j][:, u, :], ident[:]
                     )
-            words = grouped[:].bitcast(F32)[:, BANK_WORDS * b : BANK_WORDS * (b + 1)]
+            words = grouped[g][:].bitcast(F32)[:, BANK_WORDS * b : BANK_WORDS * (b + 1)]
             copy(out=words.rearrange("p (c u) -> p c u", u=2), in_=bank[:].rearrange("p u c -> p c u"))
 
-        def quantise(grouped, parts):
-            codes = quant.tile([P, 2 * ROWS], U32, name="codes", align_bytes=64)
-            scales = quant.tile([P, 2 * ROWS], U8, name="scales", align_bytes=64)
+        def quantise(g, *parts):
+            if len(quantised) == g:
+                codes = quant.tile([P, 2 * ROWS], U32, name="codes", align_bytes=64)
+                scales = quant.tile([P, 2 * ROWS], U8, name="scales", align_bytes=64)
+                quantised.append((codes, scales))
+            codes, scales = quantised[g]
             for first, end in parts:
                 nc.vector.quantize_mx(
                     out=codes[:, first:end].bitcast(FP8X4),
                     scales=scales[:, first:end],
-                    in_=grouped[:, 4 * first : 4 * end],
+                    in_=grouped[g][:, 4 * first : 4 * end],
                 )
-            return codes, scales
 
         def multiply(g, i):
             codes, scales = quantised[g]
@@ -121,43 +121,66 @@ def tile_moelineara_k_kernel(tc, x, W, *outs):
                 stop=(g == PASSES - 1),
             )
 
-        loads = [(g, 1) for g in range(HEAD_PASSES)]
-        loads.extend([(g, PASSES_PER_LOAD) for g in range(HEAD_PASSES, PASSES, PASSES_PER_LOAD)])
-        home = [(n, c) for n, (first_pass, count) in enumerate(loads) for c in range(count)]
+        loads = [[], []]
+        for operand in range(2):
+            first_pass = 0
+            while first_pass < PASSES:
+                single = first_pass < SINGLES + operand or first_pass == PASSES - 1
+                loads[operand].append((first_pass, 1 if single else 2))
+                first_pass += loads[operand][-1][1]
+        waiting = sorted(
+            (loads[operand][n][0], operand, n) for operand in range(2) for n in range(len(loads[operand]))
+        )
 
         products = [(g, i) for g in range(PASSES - 2) for i in range(ROW_TILES)]
         products.extend([(g, i) for i0 in (0, 2) for g in (PASSES - 2, PASSES - 1) for i in (i0, i0 + 1)])
 
-        staged = []
-        parted = []
+        pieces = [[], []]
+        row_tiles = [[] for g in range(PASSES)]
         grouped = []
         quantised = []
         done = 0
 
-        def split_up_to(end):
-            while len(parted) < min(end, PASSES):
-                n, c = home[len(parted)]
-                for ahead in range(len(staged), min(n + LOADS_AHEAD + 1, len(loads))):
-                    staged.append(load(loads[ahead][0], loads[ahead][1]))
-                parted.append(split_words(staged[n][c]))
+        def write_loads(g):
+            while waiting:
+                first_pass, operand, n = waiting[0]
+                if n >= STAGE_BUFS:
+                    old_first, old_count = loads[operand][n - STAGE_BUFS]
+                    if old_first + old_count > g:
+                        break
+                load(operand, first_pass, loads[operand][n][1])
+                waiting.remove(waiting[0])
 
-        split_up_to(1)
+        write_loads(0)
+        split_words(0, 0)
+        split_words(1, 0)
+        ready = 1
         for g in range(PASSES):
             last = g == PASSES - 1
-            if g > 0:
-                quantised.append(quantise(grouped[g - 1], [(0, 2 * ROWS)]))
+            if len(quantised) < g:
+                quantise(g - 1, (0, 2 * ROWS))
             grouped.append(group.tile([P, 2 * ROWS * 4], BF16, name="grouped", align_bytes=64))
             for b in (2, 3, 0, 1) if last else range(BANKS_PASS):
-                by_vector = b == VECTOR_BANK and g % 2 == 1
-                copy = nc.vector.tensor_copy if by_vector else nc.scalar.copy
-                transpose_bank(parted[g], b, grouped[g], copy)
-            split_up_to(g + (2 if g < EARLY else 3))
+                by_vector = b == VECTOR_BANK and g % 2 == 1 and g >= EARLY
+                transpose_bank(g, b, nc.vector.tensor_copy if by_vector else nc.scalar.copy)
+            if g < EARLY:
+                write_loads(ready)
+                split_words(0, g + 1)
+                quantise(g, (0, ROWS))
+                split_words(1, g + 1)
+                quantise(g, (ROWS, 2 * ROWS))
+                ready += 1
+            while EARLY <= g and ready < min(g + 3, PASSES):
+                write_loads(ready)
+                split_words(0, ready)
+                split_words(1, ready)
+                ready += 1
             if g > 0:
                 count = ROW_TILES - 1 if LATER <= g < LATER + ROW_TILES else ROW_TILES
                 for pass_no, i in products[done : done + count]:
                     multiply(pass_no, i)
                 done += count
-        quantised.append(quantise(grouped[PASSES - 1], [(ROWS, 2 * ROWS), (0, 2 * P), (2 * P, ROWS)]))
+        quantise(PASSES - 1, (ROWS, 2 * ROWS), (0, 2 * P), (2 * P, ROWS))
         for pass_no, i in products[done:]:
             multiply(pass_no, i)
 

@@ -28,6 +28,9 @@ STAGE_BUFS = 8
 EARLY = 8
 LATER = 5
 
+SHIFT_UNIT = 64
+SHIFTS = [(0, 64), (128, 192)]
+
 VECTOR_BANK = 1
 
 FLOPS = 2 * ROWS * ROWS * D
@@ -95,28 +98,33 @@ def tile_moelineara_k_kernel(tc, x, W, *outs):
             words = grouped[g][:].bitcast(F32)[:, BANK_WORDS * b : BANK_WORDS * (b + 1)]
             copy(out=words.rearrange("p (c u) -> p c u", u=2), in_=bank[:].rearrange("p u c -> p c u"))
 
-        def quantise(g, *parts):
-            if len(quantised) == g:
-                codes = quant.tile([P, 2 * ROWS], U32, name="codes", align_bytes=64)
-                scales = quant.tile([P, 2 * ROWS], U8, name="scales", align_bytes=64)
-                quantised.append((codes, scales))
-            codes, scales = quantised[g]
+        def quantise(g, operand, *parts):
+            if operand not in quantised[g]:
+                words = quant.tile([P, SHIFT_UNIT + ROWS], U32, name="words%d" % operand, align_bytes=256)
+                plane = quant.tile([P, 4 * SHIFT_UNIT + ROWS], U8, name="scales%d" % operand, align_bytes=256)
+                word_shift, scale_shift = SHIFTS[operand]
+                quantised[g][operand] = (
+                    words[:, word_shift // 4 : word_shift // 4 + ROWS],
+                    plane[:, scale_shift : scale_shift + ROWS],
+                )
+            codes, scales = quantised[g][operand]
             for first, end in parts:
                 nc.vector.quantize_mx(
                     out=codes[:, first:end].bitcast(FP8X4),
                     scales=scales[:, first:end],
-                    in_=grouped[g][:, 4 * first : 4 * end],
+                    in_=grouped[g][:, 4 * (ROWS * operand + first) : 4 * (ROWS * operand + end)],
                 )
 
         def multiply(g, i):
-            codes, scales = quantised[g]
+            x_codes, x_scales = quantised[g][0]
+            w_codes, w_scales = quantised[g][1]
             tokens = slice(P * i, P * (i + 1))
             nc.tensor.matmul_mx(
                 out=acc[i][:],
-                lhsT=codes[:, tokens].bitcast(FP8X4),
-                lhsT_scale=scales[:, tokens],
-                rhs=codes[:, ROWS : 2 * ROWS].bitcast(FP8X4),
-                rhs_scale=scales[:, ROWS : 2 * ROWS],
+                lhsT=x_codes[:, tokens].bitcast(FP8X4),
+                lhsT_scale=x_scales[:, tokens],
+                rhs=w_codes.bitcast(FP8X4),
+                rhs_scale=w_scales,
                 start=(g == 0),
                 stop=(g == PASSES - 1),
             )
@@ -138,7 +146,7 @@ def tile_moelineara_k_kernel(tc, x, W, *outs):
         pieces = [[], []]
         row_tiles = [[] for g in range(PASSES)]
         grouped = []
-        quantised = []
+        quantised = [{} for g in range(PASSES)]
         done = 0
 
         def write_loads(g):
@@ -157,8 +165,9 @@ def tile_moelineara_k_kernel(tc, x, W, *outs):
         ready = 1
         for g in range(PASSES):
             last = g == PASSES - 1
-            if len(quantised) < g:
-                quantise(g - 1, (0, 2 * ROWS))
+            if g > EARLY:
+                quantise(g - 1, 0, (0, ROWS))
+                quantise(g - 1, 1, (0, ROWS))
             grouped.append(group.tile([P, 2 * ROWS * 4], BF16, name="grouped", align_bytes=64))
             for b in (2, 3, 0, 1) if last else range(BANKS_PASS):
                 by_vector = b == VECTOR_BANK and g % 2 == 1 and g >= EARLY
@@ -166,9 +175,9 @@ def tile_moelineara_k_kernel(tc, x, W, *outs):
             if g < EARLY:
                 write_loads(ready)
                 split_words(0, g + 1)
-                quantise(g, (0, ROWS))
+                quantise(g, 0, (0, ROWS))
                 split_words(1, g + 1)
-                quantise(g, (ROWS, 2 * ROWS))
+                quantise(g, 1, (0, ROWS))
                 ready += 1
             while EARLY <= g and ready < min(g + 3, PASSES):
                 write_loads(ready)
@@ -180,7 +189,8 @@ def tile_moelineara_k_kernel(tc, x, W, *outs):
                 for pass_no, i in products[done : done + count]:
                     multiply(pass_no, i)
                 done += count
-        quantise(PASSES - 1, (ROWS, 2 * ROWS), (0, 2 * P), (2 * P, ROWS))
+        quantise(PASSES - 1, 1, (0, ROWS))
+        quantise(PASSES - 1, 0, (0, 2 * P), (2 * P, ROWS))
         for pass_no, i in products[done:]:
             multiply(pass_no, i)
 

from contextlib import ExitStack

import concourse.mybir as mybir
from concourse.masks import make_identity

BF16 = mybir.dt.bfloat16
F32 = mybir.dt.float32
U32 = mybir.dt.uint32
U8 = mybir.dt.uint8
FP8X4 = mybir.dt.float8_e4m3fn_x4

P = 128
D = 16384
ROWS = 512
EXPERTS = 8
RANK = 64
ROW_TILES = ROWS // P

D_PASS = 4 * P
PASSES = D // D_PASS
WORDS_PASS = D_PASS // 2
BANK_WORDS = 512
BANKS_PASS = 2 * ROWS * WORDS_PASS // (P * BANK_WORDS)

SINGLES = 3
STAGE_BUFS = 8

EARLY = 8
LATER = 5

SHIFT_UNIT = 64
SHIFTS = [(0, 64), (128, 192)]

VECTOR_BANK = 1

FLOPS = 2 * ROWS * ROWS * D


def tile_moelineara_k_kernel(tc, x, W, *outs):
    nc = tc.nc

    x_rows = x.flatten_outer_dims().rearrange("(p i) d -> p i d", i=ROW_TILES)
    w_rows = W.flatten_outer_dims().rearrange("(j p) d -> p j d", p=P)

    with ExitStack() as ctx:
        ctx.enter_context(tc.manual_schedule())
        fixed = ctx.enter_context(tc.tile_pool(name="fixed", bufs=1))
        stage = ctx.enter_context(tc.tile_pool(name="stage", bufs=STAGE_BUFS))
        split = ctx.enter_context(tc.tile_pool(name="split", bufs=4))
        group = ctx.enter_context(tc.tile_pool(name="group", bufs=3))
        quant = ctx.enter_context(tc.tile_pool(name="quant", bufs=4))
        turned = ctx.enter_context(tc.psum_pool(name="turned", bufs=BANKS_PASS))
        sums = ctx.enter_context(tc.psum_pool(name="sums", bufs=1))

        ident = fixed.tile([P, P], F32, name="ident")
        make_identity(nc, ident[:])

        acc = [sums.tile([P, ROWS], F32, name="acc%d" % i) for i in range(ROW_TILES)]

        def load(operand, first_pass, count):
            rows = (x_rows, w_rows)[operand]
            columns = slice(first_pass * D_PASS, (first_pass + count) * D_PASS)
            if first_pass == 0:
                staged = [
                    fixed.tile([P, 2, D_PASS], BF16, name="first%d_%d" % (operand, j)) for j in (0, 2)
                ]
            else:
                staged = [stage.tile([P, ROW_TILES, count * D_PASS], BF16, name="stage%d" % operand)]
            tiles = ROW_TILES // len(staged)
            for n, piece in enumerate(staged):
                nc.sync.dma_start(out=piece[:], in_=rows[:, tiles * n : tiles * (n + 1), columns])
            for c in range(count):
                words = slice(WORDS_PASS * c, WORDS_PASS * (c + 1))
                pieces[operand].append([piece[:].bitcast(F32)[:, :, words] for piece in staged])

        def split_words(operand, g):
            for n, words in enumerate(pieces[operand][g]):
                tiles = words.shape[1]
                if g == 0:
                    parted = fixed.tile(
                        [P, tiles, 2, P], F32, name="split%d_%d" % (operand, n), align_bytes=64
                    )
                else:
                    parted = split.tile([P, tiles, 2, P], F32, name="split%d" % operand, align_bytes=64)
                nc.vector.tensor_copy(
                    out=parted[:].rearrange("p j u (s w) -> p j u s w", w=8),
                    in_=words.rearrange("p j (s u w) -> p j u s w", u=2, w=8),
                )
                row_tiles[g].extend([parted[:, j, :, :] for j in range(tiles)])

        def transpose_bank(g, b, copy):
            bank = turned.tile([P, 2, 2 * P], F32, name="bank")
            for j in range(2):
                for u in range(2):
                    nc.tensor.transpose(
                        bank[:, u, P * j : P * (j + 1)], row_tiles[g][2 * b + j][:, u, :], ident[:]
                    )
            words = grouped[g][:].bitcast(F32)[:, BANK_WORDS * b : BANK_WORDS * (b + 1)]
            copy(out=words.rearrange("p (c u) -> p c u", u=2), in_=bank[:].rearrange("p u c -> p c u"))

        def quantise(g, operand, *parts):
            if operand not in quantised[g]:
                words = quant.tile([P, SHIFT_UNIT + ROWS], U32, name="words%d" % operand, align_bytes=256)
                plane = quant.tile([P, 4 * SHIFT_UNIT + ROWS], U8, name="scales%d" % operand, align_bytes=256)
                word_shift, scale_shift = SHIFTS[operand]
                quantised[g][operand] = (
                    words[:, word_shift // 4 : word_shift // 4 + ROWS],
                    plane[:, scale_shift : scale_shift + ROWS],
                )
            codes, scales = quantised[g][operand]
            for first, end in parts:
                nc.vector.quantize_mx(
                    out=codes[:, first:end].bitcast(FP8X4),
                    scales=scales[:, first:end],
                    in_=grouped[g][:, 4 * (ROWS * operand + first) : 4 * (ROWS * operand + end)],
                )

        def multiply(g, i):
            x_codes, x_scales = quantised[g][0]
            w_codes, w_scales = quantised[g][1]
            tokens = slice(P * i, P * (i + 1))
            nc.tensor.matmul_mx(
                out=acc[i][:],
                lhsT=x_codes[:, tokens].bitcast(FP8X4),
                lhsT_scale=x_scales[:, tokens],
                rhs=w_codes.bitcast(FP8X4),
                rhs_scale=w_scales,
                start=(g == 0),
                stop=(g == PASSES - 1),
            )

        loads = [[], []]
        for operand in range(2):
            first_pass = 0
            while first_pass < PASSES:
                single = first_pass < SINGLES + operand or first_pass == PASSES - 1
                loads[operand].append((first_pass, 1 if single else 2))
                first_pass += loads[operand][-1][1]
        waiting = sorted(
            (loads[operand][n][0], operand, n) for operand in range(2) for n in range(len(loads[operand]))
        )

        products = [(g, i) for g in range(PASSES - 2) for i in range(ROW_TILES)]
        products.extend([(g, i) for i0 in (0, 2) for g in (PASSES - 2, PASSES - 1) for i in (i0, i0 + 1)])

        pieces = [[], []]
        row_tiles = [[] for g in range(PASSES)]
        grouped = []
        quantised = [{} for g in range(PASSES)]
        done = 0

        def write_loads(g):
            while waiting:
                first_pass, operand, n = waiting[0]
                if n >= STAGE_BUFS:
                    old_first, old_count = loads[operand][n - STAGE_BUFS]
                    if old_first + old_count > g:
                        break
                load(operand, first_pass, loads[operand][n][1])
                waiting.remove(waiting[0])

        write_loads(0)
        split_words(0, 0)
        split_words(1, 0)
        ready = 1
        for g in range(PASSES):
            last = g == PASSES - 1
            if g > EARLY:
                quantise(g - 1, 0, (0, ROWS))
                quantise(g - 1, 1, (0, ROWS))
            grouped.append(group.tile([P, 2 * ROWS * 4], BF16, name="grouped", align_bytes=64))
            for b in (2, 3, 0, 1) if last else range(BANKS_PASS):
                by_vector = b == VECTOR_BANK and g % 2 == 1 and g >= EARLY
                transpose_bank(g, b, nc.vector.tensor_copy if by_vector else nc.scalar.copy)
            if g < EARLY:
                write_loads(ready)
                split_words(0, g + 1)
                quantise(g, 0, (0, ROWS))
                split_words(1, g + 1)
                quantise(g, 1, (0, ROWS))
                ready += 1
            while EARLY <= g and ready < min(g + 3, PASSES):
                write_loads(ready)
                split_words(0, ready)
                split_words(1, ready)
                ready += 1
            if g > 0:
                count = ROW_TILES - 1 if LATER <= g < LATER + ROW_TILES else ROW_TILES
                for pass_no, i in products[done : done + count]:
                    multiply(pass_no, i)
                done += count
        quantise(PASSES - 1, 1, (0, ROWS))
        quantise(PASSES - 1, 0, (0, 2 * P), (2 * P, ROWS))
        for pass_no, i in products[done:]:
            multiply(pass_no, i)

        result = fixed.tile([P, EXPERTS, ROW_TILES, RANK], F32, name="result")
        last = ROW_TILES - 1
        for copy, i, first, end in (
            (nc.scalar.copy, 0, 0, EXPERTS),
            (nc.vector.tensor_copy, 1, 0, EXPERTS),
            (nc.scalar.copy, 2, 0, EXPERTS),
            (nc.vector.tensor_copy, last, 0, EXPERTS // 2),
            (nc.scalar.copy, last, EXPERTS // 2, EXPERTS),
        ):
            copy(
                out=result[:, first:end, i, :],
                in_=acc[i][:, RANK * first : RANK * end].rearrange("p (e r) -> p e r", r=RANK),
            )
        for e in range(EXPERTS):
            queue = nc.scalar if e >= EXPERTS // 2 and e % 2 == 1 else nc.sync
            queue.dma_start(
                out=outs[e].flatten_outer_dims().rearrange("(p i) r -> p i r", i=ROW_TILES),
                in_=result[:, e, :, :],
            )
